import numpy as np
import ml_dtypes


def mxq(x, axis, fmt="e4m3"):
    dtype, down = {"e4m3": (ml_dtypes.float8_e4m3fn, 7), "e5m2": (ml_dtypes.float8_e5m2, 14)}[fmt]
    v = np.moveaxis(np.asarray(x, np.float32).astype(ml_dtypes.bfloat16).astype(np.float64), axis, -1)
    blocks = v.reshape(v.shape[:-1] + (-1, 32))
    amax = np.abs(blocks).max(-1, keepdims=True)
    byte = np.maximum(np.where(amax > 0, np.frexp(amax)[1] - 1 + 127, 0) - down, 1)
    scale = np.exp2(byte - 127.0)
    codes = (blocks / scale).astype(np.float32).astype(dtype).astype(np.float64)
    return np.moveaxis((codes * scale).reshape(v.shape), -1, axis)


WIDE = False


def mx_kscale(k):
    if not WIDE:
        return np.ones(k)
    levels = np.array([10, -10, 5, -5, 0])
    if k % 512:
        return np.exp2(np.random.permutation(np.resize(levels, k // 32))).repeat(32)
    a = np.empty((k // 512, 16))
    for p in range(k // 512):
        a[p, :8] = np.random.permutation(np.resize(levels, 8))
        for g in range(8):
            far = levels[np.abs(levels - a[p, g]) >= 10]
            a[p, g + 8] = far[np.random.randint(len(far))]
    return np.exp2(a.ravel()).repeat(32)


BF16 = ml_dtypes.bfloat16


def bf(x):
    return np.asarray(x, np.float32).astype(BF16)


def f64(x):
    return np.asarray(x).astype(np.float64)


B, G, C, F, NC = 128, 3, 512, 8192, 4096
HW = G * G
P_GEM = 3.0
EPS_GEM = 1e-6
EPS_NORM = 1e-12


def l2n(v, axis):
    n = np.sqrt(np.sum(v * v, axis=axis, keepdims=True))
    return v / np.maximum(n, EPS_NORM)


def setup_inputs():
    s, t = mx_kscale(F), mx_kscale(C)
    z = np.random.standard_normal((B, HW, F))
    return {"hdn": bf(z / (1.0 + np.exp(-1.702 * z)) * s),
            "fc2_w": bf(np.random.standard_normal((F, C)) * 1.5 / np.sqrt(F) / s[:, None] * t),
            "fc2_b": bf(np.random.standard_normal(C) * 0.3 * t),
            "head_w": bf(np.random.standard_normal((C, NC)) / np.sqrt(C) / t[:, None]),
            "head_b": bf(np.random.standard_normal(NC) * 0.3)}


def reference(hdn, fc2_w, fc2_b, head_w, head_b):
    tok = (mxq(f64(hdn), 2, "e4m3") @ mxq(f64(fc2_w), 0, "e4m3")) + f64(fc2_b)
    g = np.mean(np.maximum(tok, EPS_GEM) ** P_GEM, axis=1) ** (1.0 / P_GEM)
    desc = (mxq(g, 1, "e4m3") @ mxq(f64(head_w), 0, "e4m3")) + f64(head_b)
    return l2n(desc, 1)

@@ -1,0 +1,363 @@
+from contextlib import ExitStack
+
+import concourse.mybir as mybir
+from concourse.masks import make_identity
+
+F32 = mybir.dt.float32
+BF16 = mybir.dt.bfloat16
+U32 = mybir.dt.uint32
+U8 = mybir.dt.uint8
+FP8X4 = mybir.dt.float8_e4m3fn_x4
+ALU = mybir.AluOpType
+ACT = mybir.ActivationFunctionType
+AX = mybir.AxisListType
+
+P = 128
+PACK = 4
+K_PASS = P * PACK
+TOKENS = 9
+HIDDEN = 8192
+CHANNELS = 512
+CLASSES = 4096
+PASSES = HIDDEN // K_PASS
+C_TILES = CHANNELS // P
+BANK = 512
+D_BANKS = CLASSES // BANK
+
+EPS_GEM = 1e-6
+EPS_NORM = 1e-12
+
+FLOPS = 2 * P * TOKENS * HIDDEN * CHANNELS + 2 * P * CHANNELS * CLASSES
+
+TOKEN_GROUPS = ((0, 4), (4, 4), (8, 1))
+
+UNITS = 8
+RAW_COLS = 2 * UNITS * K_PASS
+
+PIECE_COLS = 512
+FC2_PIECES = PASSES
+HEAD_PIECES = CLASSES // PIECE_COLS
+PIECES_PER_LOAD = 2
+WEIGHT_LOADS = (FC2_PIECES + HEAD_PIECES) // PIECES_PER_LOAD
+WEIGHT_BUFS = 3
+RAW_BUFS = 3
+RUN = 4
+VECTOR_COLS = 320
+POOLED_PER_ROUND = 2
+HEAD_FIRST_ROUND = 12
+FIRST_CHUNK_BEFORE_HEAD = 5
+
+
+def tile_tokenmudule_pb_k_kernel(tc, hdn, fc2_w, fc2_b, head_w, head_b, out):
+    nc = tc.nc
+
+    rounds = []
+    for first_token, n_tokens in TOKEN_GROUPS:
+        for first_pass in range(0, PASSES, UNITS // n_tokens):
+            rounds.append((first_token, n_tokens, first_pass))
+    n_rounds = len(rounds)
+    n_chunks = n_rounds // 2
+    fc2_rounds = FC2_PIECES // PIECES_PER_LOAD
+
+    with ExitStack() as ctx:
+        const = ctx.enter_context(tc.tile_pool(name="const", bufs=1))
+        raw_pool = ctx.enter_context(tc.tile_pool(name="raw", bufs=RAW_BUFS))
+        wraw_pool = ctx.enter_context(tc.tile_pool(name="wraw", bufs=WEIGHT_BUFS))
+        wgrp_pool = ctx.enter_context(tc.tile_pool(name="wgrp", bufs=3))
+        hgrp_pool = ctx.enter_context(tc.tile_pool(name="hgrp", bufs=2))
+        hq_pool = ctx.enter_context(tc.tile_pool(name="hq", bufs=2))
+        x_pool = ctx.enter_context(tc.tile_pool(name="x", bufs=C_TILES))
+        work = ctx.enter_context(tc.tile_pool(name="work", bufs=2))
+        psum = ctx.enter_context(tc.psum_pool(name="psum", bufs=4))
+        ctx.enter_context(tc.manual_schedule())
+
+        w_codes = const.tile([P, FC2_PIECES, PIECE_COLS], U32, align_bytes=64)
+        w_scales = const.tile([P, FC2_PIECES, PIECE_COLS], U8, align_bytes=64)
+        hw_codes = const.tile([P, HEAD_PIECES, PIECE_COLS], U32, align_bytes=64)
+        hw_scales = const.tile([P, HEAD_PIECES, PIECE_COLS], U8, align_bytes=64)
+        head_bias = const.tile([P, CLASSES], BF16)
+        cube_sums = [const.tile([P, CHANNELS], F32, name="cube_sum%d" % i) for i in range(2)]
+
+        ident = const.tile([P, P], F32)
+        make_identity(nc, ident[:])
+
+        one = const.tile([P, 1], F32)
+        nc.vector.memset(one[:], 1.0)
+        warm_ln = const.tile([P, 1], F32)
+        nc.scalar.activation(out=warm_ln[:], in_=one[:], func=ACT.Ln)
+
+        bias_rows = const.tile([P, CHANNELS], BF16)
+        nc.vector.memset(bias_rows[:], 0.0)
+        nc.sync.dma_start(out=bias_rows[0:1, :], in_=fc2_b.unsqueeze(0))
+        bias_rows32 = const.tile([P, CHANNELS], F32)
+        nc.vector.tensor_copy(out=bias_rows32[:], in_=bias_rows[:])
+        tok_bias = const.tile([P, C_TILES], F32)
+
+        def transpose_bias():
+            bias_t = psum.tile([P, C_TILES, P], F32, tag="xt")
+            for j in range(C_TILES):
+                nc.tensor.transpose(bias_t[:, j, :], bias_rows32[:, j:CHANNELS:C_TILES], ident[:])
+            nc.vector.tensor_copy(out=tok_bias[:], in_=bias_t[:, :, 0])
+
+        raw_of = {}
+        wraw_of = {}
+
+        def load_hidden(chunk):
+            first_token, n_tokens, first_pass = rounds[2 * chunk]
+            span = RAW_COLS // n_tokens
+            k0 = first_pass * K_PASS
+            raw = raw_pool.tile([P, RAW_COLS], BF16, tag="raw")
+            for i in range(n_tokens):
+                nc.sync.dma_start(
+                    out=raw[:, i * span : (i + 1) * span],
+                    in_=hdn[:, first_token + i, k0 : k0 + span],
+                )
+            raw_of[chunk] = raw
+
+        def load_weights(load):
+            wraw = wraw_pool.tile([P, PIECES_PER_LOAD * PACK * PIECE_COLS], BF16, tag="wraw")
+            if load < fc2_rounds:
+                rows = fc2_w[load * 2 * K_PASS : (load + 1) * 2 * K_PASS, :]
+                nc.sync.dma_start(
+                    out=wraw[:].rearrange("p (s x) -> p s x", s=2),
+                    in_=rows.rearrange("(s p t) c -> p s (t c)", s=2, p=P, t=PACK),
+                )
+            else:
+                c0 = (load - fc2_rounds) * PIECES_PER_LOAD * PIECE_COLS
+                cols = head_w[:, c0 : c0 + PIECES_PER_LOAD * PIECE_COLS]
+                nc.sync.dma_start(
+                    out=wraw[:].rearrange("p (j n) -> p j n", j=PACK),
+                    in_=cols.rearrange("(p j) n -> p j n", p=P),
+                )
+            wraw_of[load] = wraw
+
+        wgrouped_of = {}
+
+        def regroup_piece(piece):
+            load, half = divmod(piece, PIECES_PER_LOAD)
+            wraw = wraw_of[load]
+            if piece < FC2_PIECES:
+                src = wraw[:, half * PACK * PIECE_COLS : (half + 1) * PACK * PIECE_COLS].rearrange(
+                    "p (t c) -> p t c", t=PACK
+                )
+            else:
+                src = wraw[:].rearrange("p (t n) -> p t n", t=PACK)[
+                    :, :, half * PIECE_COLS : (half + 1) * PIECE_COLS
+                ]
+            wgrouped = wgrp_pool.tile([P, PIECE_COLS, PACK], BF16, tag="wgrouped", align_bytes=64)
+            src_runs = src.rearrange("p t (c i) -> p c t i", i=RUN)
+            if piece < FC2_PIECES:
+                dst_runs = wgrouped[:].rearrange("p (i m) t -> p m t i", i=C_TILES)
+            else:
+                dst_runs = wgrouped[:].rearrange("p (c i) t -> p c t i", i=RUN)
+            split = VECTOR_COLS // RUN
+            nc.vector.tensor_copy(out=dst_runs[:, 0:split, :, :], in_=src_runs[:, 0:split, :, :])
+            nc.scalar.copy(out=dst_runs[:, split:, :, :], in_=src_runs[:, split:, :, :])
+            wgrouped_of[piece] = wgrouped
+            if half == PIECES_PER_LOAD - 1 and load + WEIGHT_BUFS < fc2_rounds:
+                load_weights(load + WEIGHT_BUFS)
+
+        def quantise_piece(piece):
+            if piece < FC2_PIECES:
+                codes, scales = w_codes[:, piece, :], w_scales[:, piece, :]
+            else:
+                codes, scales = hw_codes[:, piece - FC2_PIECES, :], hw_scales[:, piece - FC2_PIECES, :]
+            nc.vector.quantize_mx(
+                out=codes.bitcast(FP8X4),
+                scales=scales,
+                in_=wgrouped_of[piece][:].rearrange("p c t -> p (c t)"),
+            )
+
+        def pieces_before_round(r):
+            if r < fc2_rounds:
+                return (PIECES_PER_LOAD * r, PIECES_PER_LOAD * r + 1)
+            if 0 <= r - HEAD_FIRST_ROUND < HEAD_PIECES // PIECES_PER_LOAD:
+                first = FC2_PIECES + PIECES_PER_LOAD * (r - HEAD_FIRST_ROUND)
+                return (first, first + 1)
+            return ()
+
+        hgrouped_of = {}
+        hq_of = {}
+
+        def transpose_round(r):
+            first_token, n_tokens, first_pass = rounds[r]
+            raw_words = raw_of[r // 2][:].bitcast(F32)
+            words_per_token = RAW_COLS // 2 // n_tokens
+            pass_in_chunk = first_pass - rounds[2 * (r // 2)][2]
+            hgrouped = hgrp_pool.tile([P, UNITS * K_PASS], BF16, tag="hgrouped", align_bytes=64)
+            grouped_words = hgrouped[:].bitcast(F32).rearrange("p (n b u) -> p n b u", n=UNITS, u=2)
+            for pair in range(UNITS // 2):
+                xt = psum.tile([P, 2, 2, P], F32, tag="xt")
+                for a in range(2):
+                    local_pass, i = divmod(2 * pair + a, n_tokens)
+                    col = i * words_per_token + (pass_in_chunk + local_pass) * (K_PASS // 2)
+                    for u in range(2):
+                        nc.tensor.transpose(
+                            xt[:, a, u, :], raw_words[:, col + u : col + 2 * P : 2], ident[:]
+                        )
+                nc.scalar.copy(
+                    out=grouped_words[:, 2 * pair : 2 * pair + 2, :, :],
+                    in_=xt[:].rearrange("p a u b -> p a b u"),
+                )
+            hgrouped_of[r] = hgrouped
+
+        def quantise_round(r):
+            hcodes = hq_pool.tile([P, UNITS * P], U32, tag="hcodes", align_bytes=64)
+            hscales = hq_pool.tile([P, UNITS * P], U8, tag="hscales", align_bytes=64)
+            nc.vector.quantize_mx(out=hcodes[:].bitcast(FP8X4), scales=hscales[:], in_=hgrouped_of[r][:])
+            hq_of[r] = (hcodes, hscales)
+
+        acc = {}
+
+        def multiply_round(r):
+            first_token, n_tokens, first_pass = rounds[r]
+            n_cols = n_tokens * P
+            hcodes, hscales = hq_of[r]
+            if first_pass == 0:
+                for j in range(C_TILES):
+                    acc[j] = psum.tile([P, n_cols], F32, tag="acc", name="acc%d" % j)
+            for j in range(C_TILES):
+                for local_pass in range(UNITS // n_tokens):
+                    g = first_pass + local_pass
+                    nc.tensor.matmul_mx(
+                        out=acc[j][:],
+                        lhsT=w_codes[:, g, j * P : (j + 1) * P].bitcast(FP8X4),
+                        lhsT_scale=w_scales[:, g, j * P : (j + 1) * P],
+                        rhs=hcodes[:, local_pass * n_cols : (local_pass + 1) * n_cols].bitcast(FP8X4),
+                        rhs_scale=hscales[:, local_pass * n_cols : (local_pass + 1) * n_cols],
+                        start=(g == 0),
+                        stop=(g == PASSES - 1),
+                    )
+
+        def clamp(j, x):
+            nc.vector.tensor_scalar(
+                out=x, in0=acc[j][:], scalar1=tok_bias[:, j : j + 1], scalar2=EPS_GEM, op0=ALU.add, op1=ALU.max
+            )
+
+        def cube(x):
+            x2 = work.tile([P, BANK], F32, tag="x2")
+            nc.scalar.activation(out=x2[:], in_=x[:], func=ACT.Square)
+            x3 = work.tile([P, BANK], F32, tag="x3")
+            nc.vector.tensor_tensor(out=x3[:], in0=x2[:], in1=x[:], op=ALU.mult)
+            return x3
+
+        def pool_bank(x, n_tokens, dest):
+            x3 = cube(x)
+            nc.vector.tensor_reduce(
+                out=dest, in_=x3[:].rearrange("p (i b) -> p b i", i=n_tokens), axis=AX.X, op=ALU.add
+            )
+
+        load_weights(0)
+        load_hidden(0)
+        load_weights(1)
+        load_weights(2)
+        load_hidden(1)
+        for piece in pieces_before_round(0):
+            regroup_piece(piece)
+        for piece in pieces_before_round(0):
+            quantise_piece(piece)
+
+        group = 0
+        clamped = []
+        closed_at = 0
+
+        def pool_banks(first):
+            for j in range(max(first, 0), min(first + POOLED_PER_ROUND, len(clamped))):
+                pool_bank(clamped[j], rounds[closed_at - 1][1], cube_sums[group - 1][:, j * P : (j + 1) * P])
+
+        for r in range(n_rounds):
+            transpose_round(r)
+            if r == 0:
+                transpose_bias()
+            if r >= 1:
+                multiply_round(r - 1)
+            quantise_round(r)
+            if r >= 1 and rounds[r][2] == 0:
+                clamped = []
+                closed_at = r
+                for j in range(C_TILES):
+                    x = x_pool.tile([P, BANK], F32, tag="x")
+                    clamp(j, x[:])
+                    clamped.append(x)
+                group += 1
+            new_pieces = pieces_before_round(r + 1)
+            for piece in new_pieces:
+                regroup_piece(piece)
+            pool_banks(POOLED_PER_ROUND * (r - closed_at - 1))
+            for piece in new_pieces:
+                quantise_piece(piece)
+            if r % 2 == 0 and r // 2 + 2 < n_chunks:
+                chunk = r // 2 + 2
+                load_hidden(chunk)
+                if chunk >= FIRST_CHUNK_BEFORE_HEAD:
+                    load_weights(fc2_rounds + chunk - FIRST_CHUNK_BEFORE_HEAD)
+                if chunk == n_chunks - 1:
+                    nc.sync.dma_start(out=head_bias[:], in_=head_b.partition_broadcast(P))
+
+        multiply_round(n_rounds - 1)
+        pool_banks(POOLED_PER_ROUND * (n_rounds - closed_at - 1))
+        both = const.tile([P, CHANNELS], F32)
+        nc.vector.tensor_tensor(out=both[:], in0=cube_sums[0][:], in1=cube_sums[1][:], op=ALU.add)
+        x = x_pool.tile([P, BANK], F32, tag="x")
+        x2 = work.tile([P, BANK], F32, tag="x2")
+        x3 = work.tile([P, BANK], F32, tag="x3")
+        total = const.tile([P, CHANNELS], F32)
+        for j in range(C_TILES + 1):
+            if j < C_TILES:
+                cols = slice(j * P, (j + 1) * P)
+                clamp(j, x[:, cols])
+                nc.scalar.activation(out=x2[:, cols], in_=x[:, cols], func=ACT.Square)
+            if j >= 1:
+                cols = slice((j - 1) * P, j * P)
+                nc.vector.tensor_tensor(out=x3[:, cols], in0=x2[:, cols], in1=x[:, cols], op=ALU.mult)
+                nc.vector.tensor_tensor(out=total[:, cols], in0=x3[:, cols], in1=both[:, cols], op=ALU.add)
+        log_mean = const.tile([P, CHANNELS], F32)
+        nc.scalar.activation(out=log_mean[:], in_=total[:], func=ACT.Ln, scale=1.0 / TOKENS)
+        g_grouped = const.tile([P, P, PACK], BF16, align_bytes=64)
+        nc.scalar.activation(
+            out=g_grouped[:],
+            in_=log_mean[:].rearrange("p (j b) -> p b j", j=PACK),
+            func=ACT.Exp,
+            scale=1.0 / 3.0,
+        )
+        warm_sqrt = const.tile([P, 1], F32)
+        nc.scalar.activation(out=warm_sqrt[:], in_=one[:], func=ACT.Sqrt)
+        g_codes = const.tile([P, P], U32, align_bytes=64)
+        g_scales = const.tile([P, P], U8, align_bytes=64)
+        nc.vector.quantize_mx(
+            out=g_codes[:].bitcast(FP8X4), scales=g_scales[:], in_=g_grouped[:].rearrange("p b j -> p (b j)")
+        )
+
+        d = const.tile([P, CLASSES], F32)
+        squares = const.tile([P, D_BANKS], F32)
+        for n in range(D_BANKS):
+            cols = slice(n * BANK, (n + 1) * BANK)
+            d_bank = psum.tile([P, BANK], F32, tag=("acc" if n < 4 else "xt"), name="d_bank")
+            nc.tensor.matmul_mx(
+                out=d_bank[:],
+                lhsT=g_codes[:].bitcast(FP8X4),
+                lhsT_scale=g_scales[:],
+                rhs=hw_codes[:, n, :].bitcast(FP8X4),
+                rhs_scale=hw_scales[:, n, :],
+                start=True,
+                stop=True,
+            )
+            nc.vector.tensor_tensor(out=d[:, cols], in0=d_bank[:], in1=head_bias[:, cols], op=ALU.add)
+            d2 = work.tile([P, BANK], F32, tag="x2")
+            nc.scalar.activation(out=d2[:], in_=d[:, cols], func=ACT.Square, accum_out=squares[:, n : n + 1])
+        norm = const.tile([P, 1], F32)
+        nc.vector.tensor_reduce(out=norm[:], in_=squares[:], axis=AX.X, op=ALU.add)
+        nc.scalar.activation(out=norm[:], in_=norm[:], func=ACT.Sqrt)
+        nc.vector.tensor_scalar(out=norm[:], in0=norm[:], scalar1=EPS_NORM, scalar2=None, op0=ALU.max)
+        inv_norm = const.tile([P, 1], F32)
+        nc.vector.reciprocal(out=inv_norm[:], in_=norm[:])
+        for n in range(D_BANKS):
+            cols = slice(n * BANK, (n + 1) * BANK)
+            if n % 2 == 0:
+                nc.vector.tensor_scalar(
+                    out=d[:, cols], in0=d[:, cols], scalar1=inv_norm[:], scalar2=None, op0=ALU.mult
+                )
+            else:
+                nc.scalar.activation(out=d[:, cols], in_=d[:, cols], func=ACT.Copy, scale=inv_norm[:])
+                both_cols = slice((n - 1) * BANK, (n + 1) * BANK)
+                nc.sync.dma_start(out=out[:, both_cols], in_=d[:, both_cols])

@@ -25,6 +25,7 @@ BANK = 512
 D_BANKS = CLASSES // BANK
 
 EPS_GEM = 1e-6
+MIN_CUBE = EPS_GEM**3 / TOKENS
 EPS_NORM = 1e-12
 
 FLOPS = 2 * P * TOKENS * HIDDEN * CHANNELS + 2 * P * CHANNELS * CLASSES
@@ -43,7 +44,6 @@ WEIGHT_BUFS = 3
 RAW_BUFS = 3
 RUN = 4
 VECTOR_COLS = 320
-POOLED_PER_ROUND = 2
 HEAD_FIRST_ROUND = 12
 FIRST_CHUNK_BEFORE_HEAD = 5
 
@@ -66,7 +66,7 @@ def tile_tokenmudule_pb_k_kernel(tc, hdn, fc2_w, fc2_b, head_w, head_b, out):
         wgrp_pool = ctx.enter_context(tc.tile_pool(name="wgrp", bufs=3))
         hgrp_pool = ctx.enter_context(tc.tile_pool(name="hgrp", bufs=2))
         hq_pool = ctx.enter_context(tc.tile_pool(name="hq", bufs=2))
-        x_pool = ctx.enter_context(tc.tile_pool(name="x", bufs=C_TILES))
+        cube_pool = ctx.enter_context(tc.tile_pool(name="cubes", bufs=1))
         work = ctx.enter_context(tc.tile_pool(name="work", bufs=2))
         psum = ctx.enter_context(tc.psum_pool(name="psum", bufs=4))
         ctx.enter_context(tc.manual_schedule())
@@ -76,15 +76,18 @@ def tile_tokenmudule_pb_k_kernel(tc, hdn, fc2_w, fc2_b, head_w, head_b, out):
         hw_codes = const.tile([P, HEAD_PIECES, PIECE_COLS], U32, align_bytes=64)
         hw_scales = const.tile([P, HEAD_PIECES, PIECE_COLS], U8, align_bytes=64)
         head_bias = const.tile([P, CLASSES], BF16)
-        cube_sums = [const.tile([P, CHANNELS], F32, name="cube_sum%d" % i) for i in range(2)]
+        cube_sum = const.tile([P, C_TILES, 2 * P], F32)
 
         ident = const.tile([P, P], F32)
         make_identity(nc, ident[:])
 
         one = const.tile([P, 1], F32)
         nc.vector.memset(one[:], 1.0)
-        warm_ln = const.tile([P, 1], F32)
-        nc.scalar.activation(out=warm_ln[:], in_=one[:], func=ACT.Ln)
+        warm_sqrt = const.tile([P, 1], F32)
+        nc.scalar.activation(out=warm_sqrt[:], in_=one[:], func=ACT.Sqrt)
+        third = const.tile([P, CHANNELS], F32)
+        nc.gpsimd.memset(third[:], 1.0)
+        nc.gpsimd.tensor_scalar(out=third[:], in0=third[:], scalar1=1.0 / 3.0, scalar2=0.0, op0=ALU.mult, op1=ALU.add)
 
         bias_rows = const.tile([P, CHANNELS], BF16)
         nc.vector.memset(bias_rows[:], 0.0)
@@ -92,12 +95,16 @@ def tile_tokenmudule_pb_k_kernel(tc, hdn, fc2_w, fc2_b, head_w, head_b, out):
         bias_rows32 = const.tile([P, CHANNELS], F32)
         nc.vector.tensor_copy(out=bias_rows32[:], in_=bias_rows[:])
         tok_bias = const.tile([P, C_TILES], F32)
+        tok_bias_third = const.tile([P, C_TILES], F32)
 
         def transpose_bias():
             bias_t = psum.tile([P, C_TILES, P], F32, tag="xt")
             for j in range(C_TILES):
                 nc.tensor.transpose(bias_t[:, j, :], bias_rows32[:, j:CHANNELS:C_TILES], ident[:])
             nc.vector.tensor_copy(out=tok_bias[:], in_=bias_t[:, :, 0])
+            nc.vector.tensor_scalar(
+                out=tok_bias_third[:], in0=tok_bias[:], scalar1=1.0 / 3.0, scalar2=None, op0=ALU.mult
+            )
 
         raw_of = {}
         wraw_of = {}
@@ -229,23 +236,29 @@ def tile_tokenmudule_pb_k_kernel(tc, hdn, fc2_w, fc2_b, head_w, head_b, out):
                         stop=(g == PASSES - 1),
                     )
 
-        def clamp(j, x):
-            nc.vector.tensor_scalar(
-                out=x, in0=acc[j][:], scalar1=tok_bias[:, j : j + 1], scalar2=EPS_GEM, op0=ALU.add, op1=ALU.max
+        def cube_bank(j, dest):
+            square = work.tile([P, BANK], F32, tag="x2")
+            cols = dest.shape[1]
+            nc.scalar.activation(
+                out=square[:, 0:cols], in_=acc[j][:], func=ACT.Square, bias=tok_bias_third[:, j : j + 1], scale=1.0 / 3.0
+            )
+            nc.vector.scalar_tensor_tensor(
+                out=dest,
+                in0=acc[j][:],
+                scalar=tok_bias[:, j : j + 1],
+                in1=square[:, 0:cols],
+                op0=ALU.add,
+                op1=ALU.mult,
             )
 
-        def cube(x):
-            x2 = work.tile([P, BANK], F32, tag="x2")
-            nc.scalar.activation(out=x2[:], in_=x[:], func=ACT.Square)
-            x3 = work.tile([P, BANK], F32, tag="x3")
-            nc.vector.tensor_tensor(out=x3[:], in0=x2[:], in1=x[:], op=ALU.mult)
-            return x3
-
-        def pool_bank(x, n_tokens, dest):
-            x3 = cube(x)
-            nc.vector.tensor_reduce(
-                out=dest, in_=x3[:].rearrange("p (i b) -> p b i", i=n_tokens), axis=AX.X, op=ALU.add
-            )
+        def add_cubes(cubes, half, first):
+            part = cubes[:, :, 2 * half * P : 2 * (half + 1) * P]
+            if first:
+                nc.vector.tensor_scalar(out=cube_sum[:], in0=part, scalar1=MIN_CUBE, scalar2=None, op0=ALU.max)
+            else:
+                nc.vector.scalar_tensor_tensor(
+                    out=cube_sum[:], in0=part, scalar=MIN_CUBE, in1=cube_sum[:], op0=ALU.max, op1=ALU.add
+                )
 
         load_weights(0)
         load_hidden(0)
@@ -258,12 +271,8 @@ def tile_tokenmudule_pb_k_kernel(tc, hdn, fc2_w, fc2_b, head_w, head_b, out):
             quantise_piece(piece)
 
         group = 0
-        clamped = []
+        cubes = None
         closed_at = 0
-
-        def pool_banks(first):
-            for j in range(max(first, 0), min(first + POOLED_PER_ROUND, len(clamped))):
-                pool_bank(clamped[j], rounds[closed_at - 1][1], cube_sums[group - 1][:, j * P : (j + 1) * P])
 
         for r in range(n_rounds):
             transpose_round(r)
@@ -273,17 +282,17 @@ def tile_tokenmudule_pb_k_kernel(tc, hdn, fc2_w, fc2_b, head_w, head_b, out):
                 multiply_round(r - 1)
             quantise_round(r)
             if r >= 1 and rounds[r][2] == 0:
-                clamped = []
+                cubes = cube_pool.tile([P, C_TILES, BANK], F32, tag="cubes")
                 closed_at = r
                 for j in range(C_TILES):
-                    x = x_pool.tile([P, BANK], F32, tag="x")
-                    clamp(j, x[:])
-                    clamped.append(x)
+                    cube_bank(j, cubes[:, j, :])
                 group += 1
             new_pieces = pieces_before_round(r + 1)
             for piece in new_pieces:
                 regroup_piece(piece)
-            pool_banks(POOLED_PER_ROUND * (r - closed_at - 1))
+            if group and r - closed_at in (1, 2):
+                half = r - closed_at - 1
+                add_cubes(cubes, half, first=(group == 1 and half == 0))
             for piece in new_pieces:
                 quantise_piece(piece)
             if r % 2 == 0 and r // 2 + 2 < n_chunks:
@@ -295,33 +304,24 @@ def tile_tokenmudule_pb_k_kernel(tc, hdn, fc2_w, fc2_b, head_w, head_b, out):
                     nc.sync.dma_start(out=head_bias[:], in_=head_b.partition_broadcast(P))
 
         multiply_round(n_rounds - 1)
-        pool_banks(POOLED_PER_ROUND * (n_rounds - closed_at - 1))
-        both = const.tile([P, CHANNELS], F32)
-        nc.vector.tensor_tensor(out=both[:], in0=cube_sums[0][:], in1=cube_sums[1][:], op=ALU.add)
-        x = x_pool.tile([P, BANK], F32, tag="x")
-        x2 = work.tile([P, BANK], F32, tag="x2")
-        x3 = work.tile([P, BANK], F32, tag="x3")
-        total = const.tile([P, CHANNELS], F32)
-        for j in range(C_TILES + 1):
-            if j < C_TILES:
-                cols = slice(j * P, (j + 1) * P)
-                clamp(j, x[:, cols])
-                nc.scalar.activation(out=x2[:, cols], in_=x[:, cols], func=ACT.Square)
-            if j >= 1:
-                cols = slice((j - 1) * P, j * P)
-                nc.vector.tensor_tensor(out=x3[:, cols], in0=x2[:, cols], in1=x[:, cols], op=ALU.mult)
-                nc.vector.tensor_tensor(out=total[:, cols], in0=x3[:, cols], in1=both[:, cols], op=ALU.add)
-        log_mean = const.tile([P, CHANNELS], F32)
-        nc.scalar.activation(out=log_mean[:], in_=total[:], func=ACT.Ln, scale=1.0 / TOKENS)
+        add_cubes(cubes, 1, first=False)
+        both = const.tile([P, C_TILES, P], F32)
+        nc.vector.tensor_tensor(out=both[:], in0=cube_sum[:, :, 0:P], in1=cube_sum[:, :, P : 2 * P], op=ALU.add)
+        last = const.tile([P, C_TILES, P], F32)
+        mean = const.tile([P, C_TILES, P], F32)
+        for j in range(C_TILES):
+            cube_bank(j, last[:, j, :])
+        for j in range(C_TILES):
+            nc.vector.scalar_tensor_tensor(
+                out=mean[:, j, :], in0=last[:, j, :], scalar=MIN_CUBE, in1=both[:, j, :], op0=ALU.max, op1=ALU.add
+            )
         g_grouped = const.tile([P, P, PACK], BF16, align_bytes=64)
-        nc.scalar.activation(
+        nc.gpsimd.tensor_tensor(
             out=g_grouped[:],
-            in_=log_mean[:].rearrange("p (j b) -> p b j", j=PACK),
-            func=ACT.Exp,
-            scale=1.0 / 3.0,
+            in0=mean[:].rearrange("p j b -> p b j"),
+            in1=third[:].rearrange("p (b j) -> p b j", j=PACK),
+            op=ALU.pow,
         )
-        warm_sqrt = const.tile([P, 1], F32)
-        nc.scalar.activation(out=warm_sqrt[:], in_=one[:], func=ACT.Sqrt)
         g_codes = const.tile([P, P], U32, align_bytes=64)
         g_scales = const.tile([P, P], U8, align_bytes=64)
         nc.vector.quantize_mx(

@@ -25,27 +25,33 @@ BANK = 512
 D_BANKS = CLASSES // BANK
 
 EPS_GEM = 1e-6
-MIN_CUBE = EPS_GEM**3 / TOKENS
 EPS_NORM = 1e-12
+MIN_CUBE = EPS_GEM**3 / TOKENS
 
 FLOPS = 2 * P * TOKENS * HIDDEN * CHANNELS + 2 * P * CHANNELS * CLASSES
 
 TOKEN_GROUPS = ((0, 4), (4, 4), (8, 1))
 
 UNITS = 8
+PASS_WORDS = K_PASS // 2
+
+CHUNK_ROUNDS = ((0,), (1,), (2, 3), (4, 5), (6, 7), (8, 9), (10, 11), (12, 13), (14, 15), (16, 17))
 RAW_COLS = 2 * UNITS * K_PASS
+RAW_BUFS = 3
 
 PIECE_COLS = 512
 FC2_PIECES = PASSES
 HEAD_PIECES = CLASSES // PIECE_COLS
-PIECES_PER_LOAD = 2
-WEIGHT_LOADS = (FC2_PIECES + HEAD_PIECES) // PIECES_PER_LOAD
-WEIGHT_BUFS = 3
-RAW_BUFS = 3
+PIECES = FC2_PIECES + HEAD_PIECES
+WEIGHT_BUFS = 6
 RUN = 4
-VECTOR_COLS = 320
-HEAD_FIRST_ROUND = 12
-FIRST_CHUNK_BEFORE_HEAD = 5
+FC2_VECTOR_RUNS = 112
+HEAD_VECTOR_RUNS = 128
+HEAD_FIRST_ROUND = 9
+HEAD_PER_ROUND = 1
+PERMUTED_A = 4
+PERMUTED_B = 6
+FIRST_PERMUTED_ROUND = 4
 
 
 def tile_tokenmudule_pb_k_kernel(tc, hdn, fc2_w, fc2_b, head_w, head_b, out):
@@ -56,14 +62,13 @@ def tile_tokenmudule_pb_k_kernel(tc, hdn, fc2_w, fc2_b, head_w, head_b, out):
         for first_pass in range(0, PASSES, UNITS // n_tokens):
             rounds.append((first_token, n_tokens, first_pass))
     n_rounds = len(rounds)
-    n_chunks = n_rounds // 2
-    fc2_rounds = FC2_PIECES // PIECES_PER_LOAD
 
     with ExitStack() as ctx:
         const = ctx.enter_context(tc.tile_pool(name="const", bufs=1))
         raw_pool = ctx.enter_context(tc.tile_pool(name="raw", bufs=RAW_BUFS))
         wraw_pool = ctx.enter_context(tc.tile_pool(name="wraw", bufs=WEIGHT_BUFS))
         wgrp_pool = ctx.enter_context(tc.tile_pool(name="wgrp", bufs=3))
+        perm_pool = ctx.enter_context(tc.tile_pool(name="perm", bufs=2))
         hgrp_pool = ctx.enter_context(tc.tile_pool(name="hgrp", bufs=2))
         hq_pool = ctx.enter_context(tc.tile_pool(name="hq", bufs=2))
         cube_pool = ctx.enter_context(tc.tile_pool(name="cubes", bufs=1))
@@ -78,20 +83,61 @@ def tile_tokenmudule_pb_k_kernel(tc, hdn, fc2_w, fc2_b, head_w, head_b, out):
         head_bias = const.tile([P, CLASSES], BF16)
         cube_sum = const.tile([P, C_TILES, 2 * P], F32)
 
+        raw_of = {}
+        wraw_of = {}
+
+        def load_hidden(chunk):
+            rs = CHUNK_ROUNDS[chunk]
+            first_token, n_tokens, first_pass = rounds[rs[0]]
+            round_cols = UNITS // n_tokens * K_PASS
+            span = len(rs) * round_cols
+            k0 = first_pass * K_PASS
+            raw = raw_pool.tile([P, RAW_COLS], BF16, tag="raw")
+            for i in range(n_tokens):
+                nc.sync.dma_start(
+                    out=raw[:, i * span : (i + 1) * span],
+                    in_=hdn[:, first_token + i, k0 : k0 + span],
+                )
+            for n, r in enumerate(rs):
+                raw_of[r] = (raw, span // 2, n * round_cols // 2)
+
+        def load_weights(piece):
+            wraw = wraw_pool.tile([P, PACK, PIECE_COLS], BF16, tag="wraw")
+            if piece < FC2_PIECES:
+                rows = fc2_w[piece * K_PASS : (piece + 1) * K_PASS, :]
+            else:
+                c0 = (piece - FC2_PIECES) * PIECE_COLS
+                rows = head_w[:, c0 : c0 + PIECE_COLS]
+            nc.sync.dma_start(out=wraw[:], in_=rows.rearrange("(p t) c -> p t c", t=PACK))
+            wraw_of[piece] = wraw
+
+        next_chunk = 0
+        next_piece = 0
+        bias_rows = const.tile([P, CHANNELS], BF16)
+        nc.vector.memset(bias_rows[:], 0.0)
+        load_hidden(0)
+        load_weights(0)
+        load_weights(1)
+        nc.sync.dma_start(out=bias_rows[0:1, :], in_=fc2_b.unsqueeze(0))
+        load_hidden(1)
+        load_weights(2)
+        load_weights(3)
+        load_hidden(2)
+        load_weights(4)
+        load_weights(5)
+        next_chunk = 3
+        next_piece = 6
+
         ident = const.tile([P, P], F32)
         make_identity(nc, ident[:])
 
         one = const.tile([P, 1], F32)
         nc.vector.memset(one[:], 1.0)
-        warm_sqrt = const.tile([P, 1], F32)
-        nc.scalar.activation(out=warm_sqrt[:], in_=one[:], func=ACT.Sqrt)
-        third = const.tile([P, CHANNELS], F32)
-        nc.gpsimd.memset(third[:], 1.0)
-        nc.gpsimd.tensor_scalar(out=third[:], in0=third[:], scalar1=1.0 / 3.0, scalar2=0.0, op0=ALU.mult, op1=ALU.add)
+        warm_ln = const.tile([P, 1], F32)
+        nc.scalar.activation(out=warm_ln[:], in_=one[:], func=ACT.Ln)
+        minus_half = const.tile([P, 1], F32)
+        nc.gpsimd.memset(minus_half[:], -0.5)
 
-        bias_rows = const.tile([P, CHANNELS], BF16)
-        nc.vector.memset(bias_rows[:], 0.0)
-        nc.sync.dma_start(out=bias_rows[0:1, :], in_=fc2_b.unsqueeze(0))
         bias_rows32 = const.tile([P, CHANNELS], F32)
         nc.vector.tensor_copy(out=bias_rows32[:], in_=bias_rows[:])
         tok_bias = const.tile([P, C_TILES], F32)
@@ -106,63 +152,21 @@ def tile_tokenmudule_pb_k_kernel(tc, hdn, fc2_w, fc2_b, head_w, head_b, out):
                 out=tok_bias_third[:], in0=tok_bias[:], scalar1=1.0 / 3.0, scalar2=None, op0=ALU.mult
             )
 
-        raw_of = {}
-        wraw_of = {}
-
-        def load_hidden(chunk):
-            first_token, n_tokens, first_pass = rounds[2 * chunk]
-            span = RAW_COLS // n_tokens
-            k0 = first_pass * K_PASS
-            raw = raw_pool.tile([P, RAW_COLS], BF16, tag="raw")
-            for i in range(n_tokens):
-                nc.sync.dma_start(
-                    out=raw[:, i * span : (i + 1) * span],
-                    in_=hdn[:, first_token + i, k0 : k0 + span],
-                )
-            raw_of[chunk] = raw
-
-        def load_weights(load):
-            wraw = wraw_pool.tile([P, PIECES_PER_LOAD * PACK * PIECE_COLS], BF16, tag="wraw")
-            if load < fc2_rounds:
-                rows = fc2_w[load * 2 * K_PASS : (load + 1) * 2 * K_PASS, :]
-                nc.sync.dma_start(
-                    out=wraw[:].rearrange("p (s x) -> p s x", s=2),
-                    in_=rows.rearrange("(s p t) c -> p s (t c)", s=2, p=P, t=PACK),
-                )
-            else:
-                c0 = (load - fc2_rounds) * PIECES_PER_LOAD * PIECE_COLS
-                cols = head_w[:, c0 : c0 + PIECES_PER_LOAD * PIECE_COLS]
-                nc.sync.dma_start(
-                    out=wraw[:].rearrange("p (j n) -> p j n", j=PACK),
-                    in_=cols.rearrange("(p j) n -> p j n", p=P),
-                )
-            wraw_of[load] = wraw
-
         wgrouped_of = {}
 
         def regroup_piece(piece):
-            load, half = divmod(piece, PIECES_PER_LOAD)
-            wraw = wraw_of[load]
-            if piece < FC2_PIECES:
-                src = wraw[:, half * PACK * PIECE_COLS : (half + 1) * PACK * PIECE_COLS].rearrange(
-                    "p (t c) -> p t c", t=PACK
-                )
-            else:
-                src = wraw[:].rearrange("p (t n) -> p t n", t=PACK)[
-                    :, :, half * PIECE_COLS : (half + 1) * PIECE_COLS
-                ]
             wgrouped = wgrp_pool.tile([P, PIECE_COLS, PACK], BF16, tag="wgrouped", align_bytes=64)
-            src_runs = src.rearrange("p t (c i) -> p c t i", i=RUN)
+            src_runs = wraw_of[piece][:].rearrange("p t (c i) -> p c t i", i=RUN)
             if piece < FC2_PIECES:
                 dst_runs = wgrouped[:].rearrange("p (i m) t -> p m t i", i=C_TILES)
+                split = FC2_VECTOR_RUNS
             else:
                 dst_runs = wgrouped[:].rearrange("p (c i) t -> p c t i", i=RUN)
-            split = VECTOR_COLS // RUN
+                split = HEAD_VECTOR_RUNS
             nc.vector.tensor_copy(out=dst_runs[:, 0:split, :, :], in_=src_runs[:, 0:split, :, :])
-            nc.scalar.copy(out=dst_runs[:, split:, :, :], in_=src_runs[:, split:, :, :])
+            if split < PIECE_COLS // RUN:
+                nc.scalar.copy(out=dst_runs[:, split:, :, :], in_=src_runs[:, split:, :, :])
             wgrouped_of[piece] = wgrouped
-            if half == PIECES_PER_LOAD - 1 and load + WEIGHT_BUFS < fc2_rounds:
-                load_weights(load + WEIGHT_BUFS)
 
         def quantise_piece(piece):
             if piece < FC2_PIECES:
@@ -176,32 +180,61 @@ def tile_tokenmudule_pb_k_kernel(tc, hdn, fc2_w, fc2_b, head_w, head_b, out):
             )
 
         def pieces_before_round(r):
-            if r < fc2_rounds:
-                return (PIECES_PER_LOAD * r, PIECES_PER_LOAD * r + 1)
-            if 0 <= r - HEAD_FIRST_ROUND < HEAD_PIECES // PIECES_PER_LOAD:
-                first = FC2_PIECES + PIECES_PER_LOAD * (r - HEAD_FIRST_ROUND)
-                return (first, first + 1)
+            if r < FC2_PIECES // 2:
+                return (2 * r, 2 * r + 1)
+            if 0 <= r - HEAD_FIRST_ROUND < HEAD_PIECES // HEAD_PER_ROUND:
+                first = FC2_PIECES + HEAD_PER_ROUND * (r - HEAD_FIRST_ROUND)
+                return tuple(range(first, first + HEAD_PER_ROUND))
             return ()
 
+        perm_of = {}
         hgrouped_of = {}
         hq_of = {}
 
+        def words_of(r, n, count):
+            n_tokens = rounds[r][1]
+            raw, token_words, word0 = raw_of[r]
+            local_pass, i = divmod(n, n_tokens)
+            start = word0 + local_pass * PASS_WORDS
+            words = raw[:, 0 : 2 * n_tokens * token_words].bitcast(F32)
+            if n_tokens == 1:
+                return words[:, start : start + count * PASS_WORDS].rearrange("p (n w) -> p n w", n=count)
+            return words.rearrange("p (i w) -> p i w", i=n_tokens)[:, i : i + count, start : start + PASS_WORDS]
+
+        def first_permuted(r):
+            if r < FIRST_PERMUTED_ROUND:
+                return UNITS
+            return UNITS - (PERMUTED_A if r < FC2_PIECES // 2 else PERMUTED_B)
+
+        def permute_round(r):
+            first = first_permuted(r)
+            if first == UNITS:
+                return
+            perm = perm_pool.tile([P, UNITS, 2, P], F32, tag="perm")
+            in_a_pass = rounds[r][1] if rounds[r][1] > 1 else UNITS
+            n = first
+            while n < UNITS:
+                count = min(in_a_pass - n % in_a_pass, UNITS - n)
+                nc.scalar.copy(
+                    out=perm[:, n : n + count, :, :],
+                    in_=words_of(r, n, count).rearrange("p n (b u) -> p n u b", u=2),
+                )
+                n += count
+            perm_of[r] = perm
+
         def transpose_round(r):
-            first_token, n_tokens, first_pass = rounds[r]
-            raw_words = raw_of[r // 2][:].bitcast(F32)
-            words_per_token = RAW_COLS // 2 // n_tokens
-            pass_in_chunk = first_pass - rounds[2 * (r // 2)][2]
             hgrouped = hgrp_pool.tile([P, UNITS * K_PASS], BF16, tag="hgrouped", align_bytes=64)
             grouped_words = hgrouped[:].bitcast(F32).rearrange("p (n b u) -> p n b u", n=UNITS, u=2)
             for pair in range(UNITS // 2):
                 xt = psum.tile([P, 2, 2, P], F32, tag="xt")
                 for a in range(2):
-                    local_pass, i = divmod(2 * pair + a, n_tokens)
-                    col = i * words_per_token + (pass_in_chunk + local_pass) * (K_PASS // 2)
+                    n = 2 * pair + a
                     for u in range(2):
-                        nc.tensor.transpose(
-                            xt[:, a, u, :], raw_words[:, col + u : col + 2 * P : 2], ident[:]
-                        )
+                        if n < first_permuted(r):
+                            column = words_of(r, n, 1)[:, 0, u:PASS_WORDS:2]
+                        else:
+                            column = perm_of[r][:, n, u, :]
+                        nc.tensor.transpose(xt[:, a, u, :], column, ident[:])
                 nc.scalar.copy(
                     out=grouped_words[:, 2 * pair : 2 * pair + 2, :, :],
                     in_=xt[:].rearrange("p a u b -> p a b u"),
@@ -236,19 +269,22 @@ def tile_tokenmudule_pb_k_kernel(tc, hdn, fc2_w, fc2_b, head_w, head_b, out):
                         stop=(g == PASSES - 1),
                     )
 
-        def cube_bank(j, dest):
-            square = work.tile([P, BANK], F32, tag="x2")
-            cols = dest.shape[1]
+        squares_of = {}
+
+        def square_bank(j):
+            square = work.tile([P, BANK], F32, tag="square")
+            cols = rounds_cols(j)
             nc.scalar.activation(
                 out=square[:, 0:cols], in_=acc[j][:], func=ACT.Square, bias=tok_bias_third[:, j : j + 1], scale=1.0 / 3.0
             )
+            squares_of[j] = square[:, 0:cols]
+
+        def rounds_cols(j):
+            return acc[j].shape[1]
+
+        def cube_bank(j, dest):
             nc.vector.scalar_tensor_tensor(
-                out=dest,
-                in0=acc[j][:],
-                scalar=tok_bias[:, j : j + 1],
-                in1=square[:, 0:cols],
-                op0=ALU.add,
-                op1=ALU.mult,
+                out=dest, in0=acc[j][:], scalar=tok_bias[:, j : j + 1], in1=squares_of[j], op0=ALU.add, op1=ALU.mult
             )
 
         def add_cubes(cubes, half, first):
@@ -260,11 +296,6 @@ def tile_tokenmudule_pb_k_kernel(tc, hdn, fc2_w, fc2_b, head_w, head_b, out):
                     out=cube_sum[:], in0=part, scalar=MIN_CUBE, in1=cube_sum[:], op0=ALU.max, op1=ALU.add
                 )
 
-        load_weights(0)
-        load_hidden(0)
-        load_weights(1)
-        load_weights(2)
-        load_hidden(1)
         for piece in pieces_before_round(0):
             regroup_piece(piece)
         for piece in pieces_before_round(0):
@@ -273,11 +304,14 @@ def tile_tokenmudule_pb_k_kernel(tc, hdn, fc2_w, fc2_b, head_w, head_b, out):
         group = 0
         cubes = None
         closed_at = 0
+        last_of_chunk = [rs[-1] for rs in CHUNK_ROUNDS]
 
         for r in range(n_rounds):
             transpose_round(r)
             if r == 0:
                 transpose_bias()
+            if r + 2 < n_rounds:
+                permute_round(r + 2)
             if r >= 1:
                 multiply_round(r - 1)
             quantise_round(r)
@@ -285,6 +319,7 @@ def tile_tokenmudule_pb_k_kernel(tc, hdn, fc2_w, fc2_b, head_w, head_b, out):
                 cubes = cube_pool.tile([P, C_TILES, BANK], F32, tag="cubes")
                 closed_at = r
                 for j in range(C_TILES):
+                    square_bank(j)
                     cube_bank(j, cubes[:, j, :])
                 group += 1
             new_pieces = pieces_before_round(r + 1)
@@ -295,13 +330,15 @@ def tile_tokenmudule_pb_k_kernel(tc, hdn, fc2_w, fc2_b, head_w, head_b, out):
                 add_cubes(cubes, half, first=(group == 1 and half == 0))
             for piece in new_pieces:
                 quantise_piece(piece)
-            if r % 2 == 0 and r // 2 + 2 < n_chunks:
-                chunk = r // 2 + 2
-                load_hidden(chunk)
-                if chunk >= FIRST_CHUNK_BEFORE_HEAD:
-                    load_weights(fc2_rounds + chunk - FIRST_CHUNK_BEFORE_HEAD)
-                if chunk == n_chunks - 1:
+            if r in last_of_chunk and next_chunk < len(CHUNK_ROUNDS):
+                load_hidden(next_chunk)
+                next_chunk += 1
+                if next_chunk == len(CHUNK_ROUNDS):
                     nc.sync.dma_start(out=head_bias[:], in_=head_b.partition_broadcast(P))
+            for piece in new_pieces:
+                if next_piece < PIECES:
+                    load_weights(next_piece)
+                    next_piece += 1
 
         multiply_round(n_rounds - 1)
         add_cubes(cubes, 1, first=False)
@@ -309,18 +346,27 @@ def tile_tokenmudule_pb_k_kernel(tc, hdn, fc2_w, fc2_b, head_w, head_b, out):
         nc.vector.tensor_tensor(out=both[:], in0=cube_sum[:, :, 0:P], in1=cube_sum[:, :, P : 2 * P], op=ALU.add)
         last = const.tile([P, C_TILES, P], F32)
         mean = const.tile([P, C_TILES, P], F32)
-        for j in range(C_TILES):
-            cube_bank(j, last[:, j, :])
-        for j in range(C_TILES):
+        log_mean = const.tile([P, C_TILES, P], F32)
+
+        def add_last(j):
             nc.vector.scalar_tensor_tensor(
                 out=mean[:, j, :], in0=last[:, j, :], scalar=MIN_CUBE, in1=both[:, j, :], op0=ALU.max, op1=ALU.add
             )
+
+        for j in range(C_TILES):
+            square_bank(j)
+            cube_bank(j, last[:, j, :])
+            if j >= 1:
+                add_last(j - 1)
+            if j >= 2:
+                nc.scalar.activation(out=log_mean[:, j - 2, :], in_=mean[:, j - 2, :], func=ACT.Ln)
+        add_last(C_TILES - 1)
+        nc.scalar.activation(
+            out=log_mean[:, C_TILES - 2 :, :], in_=mean[:, C_TILES - 2 :, :], func=ACT.Ln
+        )
         g_grouped = const.tile([P, P, PACK], BF16, align_bytes=64)
-        nc.gpsimd.tensor_tensor(
-            out=g_grouped[:],
-            in0=mean[:].rearrange("p j b -> p b j"),
-            in1=third[:].rearrange("p (b j) -> p b j", j=PACK),
-            op=ALU.pow,
+        nc.scalar.activation(
+            out=g_grouped[:], in_=log_mean[:].rearrange("p j b -> p b j"), func=ACT.Exp, scale=1.0 / 3.0
         )
         g_codes = const.tile([P, P], U32, align_bytes=64)
         g_scales = const.tile([P, P], U8, align_bytes=64)
@@ -328,7 +374,7 @@ def tile_tokenmudule_pb_k_kernel(tc, hdn, fc2_w, fc2_b, head_w, head_b, out):
             out=g_codes[:].bitcast(FP8X4), scales=g_scales[:], in_=g_grouped[:].rearrange("p b j -> p (b j)")
         )
 
-        d = const.tile([P, CLASSES], F32)
+        d = raw_pool.tile([P, CLASSES], F32, tag="raw", name="d")
         squares = const.tile([P, D_BANKS], F32)
         for n in range(D_BANKS):
             cols = slice(n * BANK, (n + 1) * BANK)
@@ -343,21 +389,22 @@ def tile_tokenmudule_pb_k_kernel(tc, hdn, fc2_w, fc2_b, head_w, head_b, out):
                 stop=True,
             )
             nc.vector.tensor_tensor(out=d[:, cols], in0=d_bank[:], in1=head_bias[:, cols], op=ALU.add)
-            d2 = work.tile([P, BANK], F32, tag="x2")
+            d2 = work.tile([P, BANK], F32, tag="square")
             nc.scalar.activation(out=d2[:], in_=d[:, cols], func=ACT.Square, accum_out=squares[:, n : n + 1])
-        norm = const.tile([P, 1], F32)
-        nc.vector.tensor_reduce(out=norm[:], in_=squares[:], axis=AX.X, op=ALU.add)
-        nc.scalar.activation(out=norm[:], in_=norm[:], func=ACT.Sqrt)
-        nc.vector.tensor_scalar(out=norm[:], in0=norm[:], scalar1=EPS_NORM, scalar2=None, op0=ALU.max)
+        norm2 = const.tile([P, 1], F32)
+        nc.vector.tensor_reduce(out=norm2[:], in_=squares[:], axis=AX.X, op=ALU.add)
+        safe2 = const.tile([P, 1], F32)
+        nc.vector.tensor_scalar(out=safe2[:], in0=norm2[:], scalar1=EPS_NORM**2, scalar2=None, op0=ALU.max)
         inv_norm = const.tile([P, 1], F32)
-        nc.vector.reciprocal(out=inv_norm[:], in_=norm[:])
+        nc.gpsimd.tensor_tensor(out=inv_norm[:], in0=safe2[:], in1=minus_half[:], op=ALU.pow)
         for n in range(D_BANKS):
             cols = slice(n * BANK, (n + 1) * BANK)
-            if n % 2 == 0:
+            if n % 3 == 1:
+                nc.scalar.activation(out=d[:, cols], in_=d[:, cols], func=ACT.Copy, scale=inv_norm[:])
+            else:
                 nc.vector.tensor_scalar(
                     out=d[:, cols], in0=d[:, cols], scalar1=inv_norm[:], scalar2=None, op0=ALU.mult
                 )
-            else:
-                nc.scalar.activation(out=d[:, cols], in_=d[:, cols], func=ACT.Copy, scale=inv_norm[:])
-                both_cols = slice((n - 1) * BANK, (n + 1) * BANK)
-                nc.sync.dma_start(out=out[:, both_cols], in_=d[:, both_cols])
+        for n in (0, 2, 1, 3, 5, 4, 6, 7):
+            cols = slice(n * BANK, (n + 1) * BANK)
+            nc.sync.dma_start(out=out[:, cols], in_=d[:, cols])

@@ -35,9 +35,8 @@ TOKEN_GROUPS = ((0, 4), (4, 4), (8, 1))
 UNITS = 8
 PASS_WORDS = K_PASS // 2
 
-CHUNK_ROUNDS = ((0,), (1,), (2, 3), (4, 5), (6, 7), (8, 9), (10, 11), (12, 13), (14, 15), (16, 17))
-RAW_COLS = 2 * UNITS * K_PASS
-RAW_BUFS = 3
+RAW_COLS = UNITS * K_PASS
+RAW_BUFS = 6
 
 PIECE_COLS = 512
 FC2_PIECES = PASSES
@@ -45,13 +44,15 @@ HEAD_PIECES = CLASSES // PIECE_COLS
 PIECES = FC2_PIECES + HEAD_PIECES
 WEIGHT_BUFS = 6
 RUN = 4
-FC2_VECTOR_RUNS = 112
+FC2_VECTOR_RUNS = 104
 HEAD_VECTOR_RUNS = 128
 HEAD_FIRST_ROUND = 9
 HEAD_PER_ROUND = 1
-PERMUTED_A = 4
-PERMUTED_B = 6
-FIRST_PERMUTED_ROUND = 4
+PERMUTED_A = (3,0)
+PERMUTED_B = (4,2)
+FIRST_PERMUTED_ROUND = 3
+LOOKAHEAD = 1
+QUANTISE_PARTS = 2
 
 
 def tile_tokenmudule_pb_k_kernel(tc, hdn, fc2_w, fc2_b, head_w, head_b, out):
@@ -83,14 +84,20 @@ def tile_tokenmudule_pb_k_kernel(tc, hdn, fc2_w, fc2_b, head_w, head_b, out):
         head_bias = const.tile([P, CLASSES], BF16)
         cube_sum = const.tile([P, C_TILES, 2 * P], F32)
 
+        def pieces_of_round(r):
+            if r < FC2_PIECES // 2:
+                return (2 * r, 2 * r + 1)
+            if 0 <= r - HEAD_FIRST_ROUND < HEAD_PIECES // HEAD_PER_ROUND:
+                first = FC2_PIECES + HEAD_PER_ROUND * (r - HEAD_FIRST_ROUND)
+                return tuple(range(first, first + HEAD_PER_ROUND))
+            return ()
+
         raw_of = {}
         wraw_of = {}
 
-        def load_hidden(chunk):
-            rs = CHUNK_ROUNDS[chunk]
-            first_token, n_tokens, first_pass = rounds[rs[0]]
-            round_cols = UNITS // n_tokens * K_PASS
-            span = len(rs) * round_cols
+        def load_hidden(r):
+            first_token, n_tokens, first_pass = rounds[r]
+            span = RAW_COLS // n_tokens
             k0 = first_pass * K_PASS
             raw = raw_pool.tile([P, RAW_COLS], BF16, tag="raw")
             for i in range(n_tokens):
@@ -98,8 +105,7 @@ def tile_tokenmudule_pb_k_kernel(tc, hdn, fc2_w, fc2_b, head_w, head_b, out):
                     out=raw[:, i * span : (i + 1) * span],
                     in_=hdn[:, first_token + i, k0 : k0 + span],
                 )
-            for n, r in enumerate(rs):
-                raw_of[r] = (raw, span // 2, n * round_cols // 2)
+            raw_of[r] = raw
 
         def load_weights(piece):
             wraw = wraw_pool.tile([P, PACK, PIECE_COLS], BF16, tag="wraw")
@@ -111,22 +117,35 @@ def tile_tokenmudule_pb_k_kernel(tc, hdn, fc2_w, fc2_b, head_w, head_b, out):
             nc.sync.dma_start(out=wraw[:], in_=rows.rearrange("(p t) c -> p t c", t=PACK))
             wraw_of[piece] = wraw
 
-        next_chunk = 0
-        next_piece = 0
         bias_rows = const.tile([P, CHANNELS], BF16)
         nc.vector.memset(bias_rows[:], 0.0)
-        load_hidden(0)
-        load_weights(0)
-        load_weights(1)
-        nc.sync.dma_start(out=bias_rows[0:1, :], in_=fc2_b.unsqueeze(0))
-        load_hidden(1)
-        load_weights(2)
-        load_weights(3)
-        load_hidden(2)
-        load_weights(4)
-        load_weights(5)
-        next_chunk = 3
-        next_piece = 6
+
+        nc.scalar.dma_start(out=bias_rows[0:1, :], in_=fc2_b.unsqueeze(0))
+
+        def load_head_bias(what):
+            nc.sync.dma_start(out=head_bias[:], in_=what.partition_broadcast(P))
+
+        queue = [(load_weights, 0)]
+        for r in range(n_rounds):
+            queue.append((load_hidden, r))
+            for piece in pieces_of_round(r):
+                if piece > 0:
+                    queue.append((load_weights, piece))
+        queue.append((load_head_bias, head_b))
+        transposed = set()
+        regrouped = set()
+
+        def issue_loads():
+            while queue:
+                load, what = queue[0]
+                if load == load_hidden and what >= RAW_BUFS and what - RAW_BUFS not in transposed:
+                    return
+                if load == load_weights and what >= WEIGHT_BUFS and what - WEIGHT_BUFS not in regrouped:
+                    return
+                load(what)
+                queue.pop(0)
+
+        issue_loads()
 
         ident = const.tile([P, P], F32)
         make_identity(nc, ident[:])
@@ -159,7 +178,7 @@ def tile_tokenmudule_pb_k_kernel(tc, hdn, fc2_w, fc2_b, head_w, head_b, out):
             src_runs = wraw_of[piece][:].rearrange("p t (c i) -> p c t i", i=RUN)
             if piece < FC2_PIECES:
                 dst_runs = wgrouped[:].rearrange("p (i m) t -> p m t i", i=C_TILES)
-                split = FC2_VECTOR_RUNS
+                split = FC2_VECTOR_RUNS if piece >= 2 else PIECE_COLS // RUN
             else:
                 dst_runs = wgrouped[:].rearrange("p (c i) t -> p c t i", i=RUN)
                 split = HEAD_VECTOR_RUNS
@@ -167,6 +186,7 @@ def tile_tokenmudule_pb_k_kernel(tc, hdn, fc2_w, fc2_b, head_w, head_b, out):
             if split < PIECE_COLS // RUN:
                 nc.scalar.copy(out=dst_runs[:, split:, :, :], in_=src_runs[:, split:, :, :])
             wgrouped_of[piece] = wgrouped
+            regrouped.add(piece)
 
         def quantise_piece(piece):
             if piece < FC2_PIECES:
@@ -179,13 +199,6 @@ def tile_tokenmudule_pb_k_kernel(tc, hdn, fc2_w, fc2_b, head_w, head_b, out):
                 in_=wgrouped_of[piece][:].rearrange("p c t -> p (c t)"),
             )
 
-        def pieces_before_round(r):
-            if r < FC2_PIECES // 2:
-                return (2 * r, 2 * r + 1)
-            if 0 <= r - HEAD_FIRST_ROUND < HEAD_PIECES // HEAD_PER_ROUND:
-                first = FC2_PIECES + HEAD_PER_ROUND * (r - HEAD_FIRST_ROUND)
-                return tuple(range(first, first + HEAD_PER_ROUND))
-            return ()
 
         perm_of = {}
         hgrouped_of = {}
@@ -193,47 +206,54 @@ def tile_tokenmudule_pb_k_kernel(tc, hdn, fc2_w, fc2_b, head_w, head_b, out):
 
         def words_of(r, n, count):
             n_tokens = rounds[r][1]
-            raw, token_words, word0 = raw_of[r]
             local_pass, i = divmod(n, n_tokens)
-            start = word0 + local_pass * PASS_WORDS
-            words = raw[:, 0 : 2 * n_tokens * token_words].bitcast(F32)
+            start = local_pass * PASS_WORDS
+            words = raw_of[r][:].bitcast(F32)
             if n_tokens == 1:
                 return words[:, start : start + count * PASS_WORDS].rearrange("p (n w) -> p n w", n=count)
             return words.rearrange("p (i w) -> p i w", i=n_tokens)[:, i : i + count, start : start + PASS_WORDS]
 
-        def first_permuted(r):
+        def permuted_units(r):
             if r < FIRST_PERMUTED_ROUND:
-                return UNITS
-            return UNITS - (PERMUTED_A if r < FC2_PIECES // 2 else PERMUTED_B)
+                return (), ()
+            by_scalar, by_vector = PERMUTED_A if r < FC2_PIECES // 2 else PERMUTED_B
+            if rounds[r - 1][2] == 0:
+                by_vector = 0
+            return range(UNITS - by_scalar, UNITS), range(UNITS - by_scalar - by_vector, UNITS - by_scalar)
 
-        def permute_round(r):
-            first = first_permuted(r)
-            if first == UNITS:
-                return
-            perm = perm_pool.tile([P, UNITS, 2, P], F32, tag="perm")
+        def permute(r, units, copy):
             in_a_pass = rounds[r][1] if rounds[r][1] > 1 else UNITS
-            n = first
-            while n < UNITS:
-                count = min(in_a_pass - n % in_a_pass, UNITS - n)
-                nc.scalar.copy(
-                    out=perm[:, n : n + count, :, :],
+            n = units[0]
+            while n <= units[-1]:
+                count = min(in_a_pass - n % in_a_pass, units[-1] + 1 - n)
+                copy(
+                    out=perm_of[r][:, n : n + count, :, :],
                     in_=words_of(r, n, count).rearrange("p n (b u) -> p n u b", u=2),
                 )
                 n += count
-            perm_of[r] = perm
+
+        def permute_round(r):
+            by_scalar, by_vector = permuted_units(r)
+            if len(by_scalar) + len(by_vector):
+                perm_of[r] = perm_pool.tile([P, UNITS, 2, P], F32, tag="perm", name="perm")
+            if len(by_vector):
+                permute(r, by_vector, nc.vector.tensor_copy)
+            if len(by_scalar):
+                permute(r, by_scalar, nc.scalar.copy)
 
         def transpose_round(r):
             hgrouped = hgrp_pool.tile([P, UNITS * K_PASS], BF16, tag="hgrouped", align_bytes=64)
             grouped_words = hgrouped[:].bitcast(F32).rearrange("p (n b u) -> p n b u", n=UNITS, u=2)
+            permuted = [n for units in permuted_units(r) for n in units]
             for pair in range(UNITS // 2):
                 xt = psum.tile([P, 2, 2, P], F32, tag="xt")
                 for a in range(2):
                     n = 2 * pair + a
                     for u in range(2):
-                        if n < first_permuted(r):
-                            column = words_of(r, n, 1)[:, 0, u:PASS_WORDS:2]
-                        else:
+                        if n in permuted:
                             column = perm_of[r][:, n, u, :]
+                        else:
+                            column = words_of(r, n, 1)[:, 0, u:PASS_WORDS:2]
                         nc.tensor.transpose(xt[:, a, u, :], column, ident[:])
                 nc.scalar.copy(
                     out=grouped_words[:, 2 * pair : 2 * pair + 2, :, :],
@@ -241,50 +261,50 @@ def tile_tokenmudule_pb_k_kernel(tc, hdn, fc2_w, fc2_b, head_w, head_b, out):
                 )
             hgrouped_of[r] = hgrouped
 
-        def quantise_round(r):
-            hcodes = hq_pool.tile([P, UNITS * P], U32, tag="hcodes", align_bytes=64)
-            hscales = hq_pool.tile([P, UNITS * P], U8, tag="hscales", align_bytes=64)
-            nc.vector.quantize_mx(out=hcodes[:].bitcast(FP8X4), scales=hscales[:], in_=hgrouped_of[r][:])
-            hq_of[r] = (hcodes, hscales)
+        def quantise_units(r, first, count):
+            if first == 0:
+                hcodes = hq_pool.tile([P, UNITS * P], U32, tag="hcodes", align_bytes=64)
+                hscales = hq_pool.tile([P, UNITS * P], U8, tag="hscales", align_bytes=64)
+                hq_of[r] = (hcodes, hscales)
+            hcodes, hscales = hq_of[r]
+            cols = slice(first * P, (first + count) * P)
+            nc.vector.quantize_mx(
+                out=hcodes[:, cols].bitcast(FP8X4),
+                scales=hscales[:, cols],
+                in_=hgrouped_of[r][:, first * K_PASS : (first + count) * K_PASS],
+            )
 
         acc = {}
 
-        def multiply_round(r):
+        def multiply_units(r, first, count):
             first_token, n_tokens, first_pass = rounds[r]
             n_cols = n_tokens * P
             hcodes, hscales = hq_of[r]
-            if first_pass == 0:
+            if first_pass == 0 and first == 0:
                 for j in range(C_TILES):
                     acc[j] = psum.tile([P, n_cols], F32, tag="acc", name="acc%d" % j)
             for j in range(C_TILES):
-                for local_pass in range(UNITS // n_tokens):
+                for local_pass in range(first // n_tokens, (first + count) // n_tokens):
                     g = first_pass + local_pass
+                    cols = slice(local_pass * n_cols, (local_pass + 1) * n_cols)
                     nc.tensor.matmul_mx(
                         out=acc[j][:],
                         lhsT=w_codes[:, g, j * P : (j + 1) * P].bitcast(FP8X4),
                         lhsT_scale=w_scales[:, g, j * P : (j + 1) * P],
-                        rhs=hcodes[:, local_pass * n_cols : (local_pass + 1) * n_cols].bitcast(FP8X4),
-                        rhs_scale=hscales[:, local_pass * n_cols : (local_pass + 1) * n_cols],
+                        rhs=hcodes[:, cols].bitcast(FP8X4),
+                        rhs_scale=hscales[:, cols],
                         start=(g == 0),
                         stop=(g == PASSES - 1),
                     )
 
-        squares_of = {}
-
-        def square_bank(j):
-            square = work.tile([P, BANK], F32, tag="square")
-            cols = rounds_cols(j)
+        def square_bank(j, square):
             nc.scalar.activation(
-                out=square[:, 0:cols], in_=acc[j][:], func=ACT.Square, bias=tok_bias_third[:, j : j + 1], scale=1.0 / 3.0
+                out=square, in_=acc[j][:], func=ACT.Square, bias=tok_bias_third[:, j : j + 1], scale=1.0 / 3.0
             )
-            squares_of[j] = square[:, 0:cols]
 
-        def rounds_cols(j):
-            return acc[j].shape[1]
-
-        def cube_bank(j, dest):
+        def cube_bank(j, square, cube):
             nc.vector.scalar_tensor_tensor(
-                out=dest, in0=acc[j][:], scalar=tok_bias[:, j : j + 1], in1=squares_of[j], op0=ALU.add, op1=ALU.mult
+                out=cube, in0=acc[j][:], scalar=tok_bias[:, j : j + 1], in1=square, op0=ALU.add, op1=ALU.mult
             )
 
         def add_cubes(cubes, half, first):
@@ -296,74 +316,73 @@ def tile_tokenmudule_pb_k_kernel(tc, hdn, fc2_w, fc2_b, head_w, head_b, out):
                     out=cube_sum[:], in0=part, scalar=MIN_CUBE, in1=cube_sum[:], op0=ALU.max, op1=ALU.add
                 )
 
-        for piece in pieces_before_round(0):
+        transpose_bias()
+        for piece in pieces_of_round(0):
             regroup_piece(piece)
-        for piece in pieces_before_round(0):
+        for piece in pieces_of_round(0):
             quantise_piece(piece)
 
         group = 0
         cubes = None
         closed_at = 0
-        last_of_chunk = [rs[-1] for rs in CHUNK_ROUNDS]
 
         for r in range(n_rounds):
             transpose_round(r)
-            if r == 0:
-                transpose_bias()
-            if r + 2 < n_rounds:
-                permute_round(r + 2)
+            if r + LOOKAHEAD < n_rounds:
+                permute_round(r + LOOKAHEAD)
             if r >= 1:
-                multiply_round(r - 1)
-            quantise_round(r)
+                multiply_units(r - 1, 0, UNITS)
+            if r < n_rounds - 1:
+                quantise_units(r, 0, UNITS)
+            else:
+                quantise_units(r, 0, UNITS // 2)
+                add_cubes(cubes, 1, first=False)
+                quantise_units(r, UNITS // 2, UNITS // 2)
             if r >= 1 and rounds[r][2] == 0:
                 cubes = cube_pool.tile([P, C_TILES, BANK], F32, tag="cubes")
                 closed_at = r
                 for j in range(C_TILES):
-                    square_bank(j)
-                    cube_bank(j, cubes[:, j, :])
+                    square = work.tile([P, BANK], F32, tag="square")
+                    square_bank(j, square[:])
+                    cube_bank(j, square[:], cubes[:, j, :])
                 group += 1
-            new_pieces = pieces_before_round(r + 1)
+                if group == 2:
+                    add_cubes(cubes, 0, first=False)
+            new_pieces = pieces_of_round(r + 1)
             for piece in new_pieces:
                 regroup_piece(piece)
-            if group and r - closed_at in (1, 2):
+            if group == 1 and r - closed_at in (1, 2):
                 half = r - closed_at - 1
-                add_cubes(cubes, half, first=(group == 1 and half == 0))
+                add_cubes(cubes, half, first=(half == 0))
             for piece in new_pieces:
                 quantise_piece(piece)
-            if r in last_of_chunk and next_chunk < len(CHUNK_ROUNDS):
-                load_hidden(next_chunk)
-                next_chunk += 1
-                if next_chunk == len(CHUNK_ROUNDS):
-                    nc.sync.dma_start(out=head_bias[:], in_=head_b.partition_broadcast(P))
-            for piece in new_pieces:
-                if next_piece < PIECES:
-                    load_weights(next_piece)
-                    next_piece += 1
+            transposed.add(r)
+            issue_loads()
 
-        multiply_round(n_rounds - 1)
-        add_cubes(cubes, 1, first=False)
+        for half in range(2):
+            multiply_units(n_rounds - 1, half * (UNITS // 2), UNITS // 2)
         both = const.tile([P, C_TILES, P], F32)
         nc.vector.tensor_tensor(out=both[:], in0=cube_sum[:, :, 0:P], in1=cube_sum[:, :, P : 2 * P], op=ALU.add)
+        last_square = const.tile([P, C_TILES, P], F32)
         last = const.tile([P, C_TILES, P], F32)
         mean = const.tile([P, C_TILES, P], F32)
         log_mean = const.tile([P, C_TILES, P], F32)
-
-        def add_last(j):
-            nc.vector.scalar_tensor_tensor(
-                out=mean[:, j, :], in0=last[:, j, :], scalar=MIN_CUBE, in1=both[:, j, :], op0=ALU.max, op1=ALU.add
-            )
-
-        for j in range(C_TILES):
-            square_bank(j)
-            cube_bank(j, last[:, j, :])
+        for j in range(C_TILES + 1):
+            if j < C_TILES:
+                square_bank(j, last_square[:, j, :])
+                cube_bank(j, last_square[:, j, :], last[:, j, :])
             if j >= 1:
-                add_last(j - 1)
-            if j >= 2:
-                nc.scalar.activation(out=log_mean[:, j - 2, :], in_=mean[:, j - 2, :], func=ACT.Ln)
-        add_last(C_TILES - 1)
-        nc.scalar.activation(
-            out=log_mean[:, C_TILES - 2 :, :], in_=mean[:, C_TILES - 2 :, :], func=ACT.Ln
-        )
+                nc.vector.scalar_tensor_tensor(
+                    out=mean[:, j - 1, :],
+                    in0=last[:, j - 1, :],
+                    scalar=MIN_CUBE,
+                    in1=both[:, j - 1, :],
+                    op0=ALU.max,
+                    op1=ALU.add,
+                )
+        nc.scalar.activation(out=log_mean[:, 0:2, :], in_=mean[:, 0:2, :], func=ACT.Ln)
+        nc.scalar.activation(out=log_mean[:, 2, :], in_=mean[:, 2, :], func=ACT.Ln)
+        nc.scalar.activation(out=log_mean[:, 3, :], in_=mean[:, 3, :], func=ACT.Ln)
         g_grouped = const.tile([P, P, PACK], BF16, align_bytes=64)
         nc.scalar.activation(
             out=g_grouped[:], in_=log_mean[:].rearrange("p j b -> p b j"), func=ACT.Exp, scale=1.0 / 3.0
@@ -374,7 +393,12 @@ def tile_tokenmudule_pb_k_kernel(tc, hdn, fc2_w, fc2_b, head_w, head_b, out):
             out=g_codes[:].bitcast(FP8X4), scales=g_scales[:], in_=g_grouped[:].rearrange("p b j -> p (b j)")
         )
 
-        d = raw_pool.tile([P, CLASSES], F32, tag="raw", name="d")
+        halves = [raw_pool.tile([P, CLASSES // 2], F32, tag="raw", name="d%d" % i) for i in range(2)]
+
+        def d(n):
+            half, bank = divmod(n, D_BANKS // 2)
+            return halves[half][:, bank * BANK : (bank + 1) * BANK]
+
         squares = const.tile([P, D_BANKS], F32)
         for n in range(D_BANKS):
             cols = slice(n * BANK, (n + 1) * BANK)
@@ -388,9 +412,9 @@ def tile_tokenmudule_pb_k_kernel(tc, hdn, fc2_w, fc2_b, head_w, head_b, out):
                 start=True,
                 stop=True,
             )
-            nc.vector.tensor_tensor(out=d[:, cols], in0=d_bank[:], in1=head_bias[:, cols], op=ALU.add)
+            nc.vector.tensor_tensor(out=d(n), in0=d_bank[:], in1=head_bias[:, cols], op=ALU.add)
             d2 = work.tile([P, BANK], F32, tag="square")
-            nc.scalar.activation(out=d2[:], in_=d[:, cols], func=ACT.Square, accum_out=squares[:, n : n + 1])
+            nc.scalar.activation(out=d2[:], in_=d(n), func=ACT.Square, accum_out=squares[:, n : n + 1])
         norm2 = const.tile([P, 1], F32)
         nc.vector.tensor_reduce(out=norm2[:], in_=squares[:], axis=AX.X, op=ALU.add)
         safe2 = const.tile([P, 1], F32)
@@ -400,11 +424,11 @@ def tile_tokenmudule_pb_k_kernel(tc, hdn, fc2_w, fc2_b, head_w, head_b, out):
         for n in range(D_BANKS):
             cols = slice(n * BANK, (n + 1) * BANK)
             if n % 3 == 1:
-                nc.scalar.activation(out=d[:, cols], in_=d[:, cols], func=ACT.Copy, scale=inv_norm[:])
+                nc.scalar.activation(out=d(n), in_=d(n), func=ACT.Copy, scale=inv_norm[:])
             else:
                 nc.vector.tensor_scalar(
-                    out=d[:, cols], in0=d[:, cols], scalar1=inv_norm[:], scalar2=None, op0=ALU.mult
+                    out=d(n), in0=d(n), scalar1=inv_norm[:], scalar2=None, op0=ALU.mult
                 )
         for n in (0, 2, 1, 3, 5, 4, 6, 7):
             cols = slice(n * BANK, (n + 1) * BANK)
-            nc.sync.dma_start(out=out[:, cols], in_=d[:, cols])
+            nc.sync.dma_start(out=out[:, cols], in_=d(n))

from contextlib import ExitStack

import concourse.mybir as mybir
from concourse.masks import make_identity

F32 = mybir.dt.float32
BF16 = mybir.dt.bfloat16
U32 = mybir.dt.uint32
U8 = mybir.dt.uint8
FP8X4 = mybir.dt.float8_e4m3fn_x4
ALU = mybir.AluOpType
ACT = mybir.ActivationFunctionType
AX = mybir.AxisListType

P = 128
PACK = 4
K_PASS = P * PACK
TOKENS = 9
HIDDEN = 8192
CHANNELS = 512
CLASSES = 4096
PASSES = HIDDEN // K_PASS
C_TILES = CHANNELS // P
BANK = 512
D_BANKS = CLASSES // BANK

EPS_GEM = 1e-6
EPS_NORM = 1e-12
MIN_CUBE = EPS_GEM**3 / TOKENS

FLOPS = 2 * P * TOKENS * HIDDEN * CHANNELS + 2 * P * CHANNELS * CLASSES

TOKEN_GROUPS = ((0, 4), (4, 4), (8, 1))

UNITS = 8
PASS_WORDS = K_PASS // 2

RAW_COLS = UNITS * K_PASS
RAW_BUFS = 6

PIECE_COLS = 512
FC2_PIECES = PASSES
HEAD_PIECES = CLASSES // PIECE_COLS
PIECES = FC2_PIECES + HEAD_PIECES
WEIGHT_BUFS = 6
RUN = 4
FC2_VECTOR_RUNS = 104
HEAD_VECTOR_RUNS = 128
HEAD_FIRST_ROUND = 9
HEAD_PER_ROUND = 1
PERMUTED_A = (3,0)
PERMUTED_B = (4,2)
FIRST_PERMUTED_ROUND = 3
LOOKAHEAD = 1
QUANTISE_PARTS = 2


def tile_tokenmudule_pb_k_kernel(tc, hdn, fc2_w, fc2_b, head_w, head_b, out):
    nc = tc.nc

    rounds = []
    for first_token, n_tokens in TOKEN_GROUPS:
        for first_pass in range(0, PASSES, UNITS // n_tokens):
            rounds.append((first_token, n_tokens, first_pass))
    n_rounds = len(rounds)

    with ExitStack() as ctx:
        const = ctx.enter_context(tc.tile_pool(name="const", bufs=1))
        raw_pool = ctx.enter_context(tc.tile_pool(name="raw", bufs=RAW_BUFS))
        wraw_pool = ctx.enter_context(tc.tile_pool(name="wraw", bufs=WEIGHT_BUFS))
        wgrp_pool = ctx.enter_context(tc.tile_pool(name="wgrp", bufs=3))
        perm_pool = ctx.enter_context(tc.tile_pool(name="perm", bufs=2))
        hgrp_pool = ctx.enter_context(tc.tile_pool(name="hgrp", bufs=2))
        hq_pool = ctx.enter_context(tc.tile_pool(name="hq", bufs=2))
        cube_pool = ctx.enter_context(tc.tile_pool(name="cubes", bufs=1))
        work = ctx.enter_context(tc.tile_pool(name="work", bufs=2))
        psum = ctx.enter_context(tc.psum_pool(name="psum", bufs=4))
        ctx.enter_context(tc.manual_schedule())

        w_codes = const.tile([P, FC2_PIECES, PIECE_COLS], U32, align_bytes=64)
        w_scales = const.tile([P, FC2_PIECES, PIECE_COLS], U8, align_bytes=64)
        hw_codes = const.tile([P, HEAD_PIECES, PIECE_COLS], U32, align_bytes=64)
        hw_scales = const.tile([P, HEAD_PIECES, PIECE_COLS], U8, align_bytes=64)
        head_bias = const.tile([P, CLASSES], BF16)
        cube_sum = const.tile([P, C_TILES, 2 * P], F32)

        def pieces_of_round(r):
            if r < FC2_PIECES // 2:
                return (2 * r, 2 * r + 1)
            if 0 <= r - HEAD_FIRST_ROUND < HEAD_PIECES // HEAD_PER_ROUND:
                first = FC2_PIECES + HEAD_PER_ROUND * (r - HEAD_FIRST_ROUND)
                return tuple(range(first, first + HEAD_PER_ROUND))
            return ()

        raw_of = {}
        wraw_of = {}

        def load_hidden(r):
            first_token, n_tokens, first_pass = rounds[r]
            span = RAW_COLS // n_tokens
            k0 = first_pass * K_PASS
            raw = raw_pool.tile([P, RAW_COLS], BF16, tag="raw")
            for i in range(n_tokens):
                nc.sync.dma_start(
                    out=raw[:, i * span : (i + 1) * span],
                    in_=hdn[:, first_token + i, k0 : k0 + span],
                )
            raw_of[r] = raw

        def load_weights(piece):
            wraw = wraw_pool.tile([P, PACK, PIECE_COLS], BF16, tag="wraw")
            if piece < FC2_PIECES:
                rows = fc2_w[piece * K_PASS : (piece + 1) * K_PASS, :]
            else:
                c0 = (piece - FC2_PIECES) * PIECE_COLS
                rows = head_w[:, c0 : c0 + PIECE_COLS]
            nc.sync.dma_start(out=wraw[:], in_=rows.rearrange("(p t) c -> p t c", t=PACK))
            wraw_of[piece] = wraw

        bias_rows = const.tile([P, CHANNELS], BF16)
        nc.vector.memset(bias_rows[:], 0.0)

        nc.scalar.dma_start(out=bias_rows[0:1, :], in_=fc2_b.unsqueeze(0))

        def load_head_bias(what):
            nc.sync.dma_start(out=head_bias[:], in_=what.partition_broadcast(P))

        queue = [(load_weights, 0)]
        for r in range(n_rounds):
            queue.append((load_hidden, r))
            for piece in pieces_of_round(r):
                if piece > 0:
                    queue.append((load_weights, piece))
        queue.append((load_head_bias, head_b))
        transposed = set()
        regrouped = set()

        def issue_loads():
            while queue:
                load, what = queue[0]
                if load == load_hidden and what >= RAW_BUFS and what - RAW_BUFS not in transposed:
                    return
                if load == load_weights and what >= WEIGHT_BUFS and what - WEIGHT_BUFS not in regrouped:
                    return
                load(what)
                queue.pop(0)

        issue_loads()

        ident = const.tile([P, P], F32)
        make_identity(nc, ident[:])

        one = const.tile([P, 1], F32)
        nc.vector.memset(one[:], 1.0)
        warm_ln = const.tile([P, 1], F32)
        nc.scalar.activation(out=warm_ln[:], in_=one[:], func=ACT.Ln)
        minus_half = const.tile([P, 1], F32)
        nc.gpsimd.memset(minus_half[:], -0.5)

        bias_rows32 = const.tile([P, CHANNELS], F32)
        nc.vector.tensor_copy(out=bias_rows32[:], in_=bias_rows[:])
        tok_bias = const.tile([P, C_TILES], F32)
        tok_bias_third = const.tile([P, C_TILES], F32)

        def transpose_bias():
            bias_t = psum.tile([P, C_TILES, P], F32, tag="xt")
            for j in range(C_TILES):
                nc.tensor.transpose(bias_t[:, j, :], bias_rows32[:, j:CHANNELS:C_TILES], ident[:])
            nc.vector.tensor_copy(out=tok_bias[:], in_=bias_t[:, :, 0])
            nc.vector.tensor_scalar(
                out=tok_bias_third[:], in0=tok_bias[:], scalar1=1.0 / 3.0, scalar2=None, op0=ALU.mult
            )

        wgrouped_of = {}

        def regroup_piece(piece):
            wgrouped = wgrp_pool.tile([P, PIECE_COLS, PACK], BF16, tag="wgrouped", align_bytes=64)
            src_runs = wraw_of[piece][:].rearrange("p t (c i) -> p c t i", i=RUN)
            if piece < FC2_PIECES:
                dst_runs = wgrouped[:].rearrange("p (i m) t -> p m t i", i=C_TILES)
                split = FC2_VECTOR_RUNS if piece >= 2 else PIECE_COLS // RUN
            else:
                dst_runs = wgrouped[:].rearrange("p (c i) t -> p c t i", i=RUN)
                split = HEAD_VECTOR_RUNS
            nc.vector.tensor_copy(out=dst_runs[:, 0:split, :, :], in_=src_runs[:, 0:split, :, :])
            if split < PIECE_COLS // RUN:
                nc.scalar.copy(out=dst_runs[:, split:, :, :], in_=src_runs[:, split:, :, :])
            wgrouped_of[piece] = wgrouped
            regrouped.add(piece)

        def quantise_piece(piece):
            if piece < FC2_PIECES:
                codes, scales = w_codes[:, piece, :], w_scales[:, piece, :]
            else:
                codes, scales = hw_codes[:, piece - FC2_PIECES, :], hw_scales[:, piece - FC2_PIECES, :]
            nc.vector.quantize_mx(
                out=codes.bitcast(FP8X4),
                scales=scales,
                in_=wgrouped_of[piece][:].rearrange("p c t -> p (c t)"),
            )


        perm_of = {}
        hgrouped_of = {}
        hq_of = {}

        def words_of(r, n, count):
            n_tokens = rounds[r][1]
            local_pass, i = divmod(n, n_tokens)
            start = local_pass * PASS_WORDS
            words = raw_of[r][:].bitcast(F32)
            if n_tokens == 1:
                return words[:, start : start + count * PASS_WORDS].rearrange("p (n w) -> p n w", n=count)
            return words.rearrange("p (i w) -> p i w", i=n_tokens)[:, i : i + count, start : start + PASS_WORDS]

        def permuted_units(r):
            if r < FIRST_PERMUTED_ROUND:
                return (), ()
            by_scalar, by_vector = PERMUTED_A if r < FC2_PIECES // 2 else PERMUTED_B
            if rounds[r - 1][2] == 0:
                by_vector = 0
            return range(UNITS - by_scalar, UNITS), range(UNITS - by_scalar - by_vector, UNITS - by_scalar)

        def permute(r, units, copy):
            in_a_pass = rounds[r][1] if rounds[r][1] > 1 else UNITS
            n = units[0]
            while n <= units[-1]:
                count = min(in_a_pass - n % in_a_pass, units[-1] + 1 - n)
                copy(
                    out=perm_of[r][:, n : n + count, :, :],
                    in_=words_of(r, n, count).rearrange("p n (b u) -> p n u b", u=2),
                )
                n += count

        def permute_round(r):
            by_scalar, by_vector = permuted_units(r)
            if len(by_scalar) + len(by_vector):
                perm_of[r] = perm_pool.tile([P, UNITS, 2, P], F32, tag="perm", name="perm")
            if len(by_vector):
                permute(r, by_vector, nc.vector.tensor_copy)
            if len(by_scalar):
                permute(r, by_scalar, nc.scalar.copy)

        def transpose_round(r):
            hgrouped = hgrp_pool.tile([P, UNITS * K_PASS], BF16, tag="hgrouped", align_bytes=64)
            grouped_words = hgrouped[:].bitcast(F32).rearrange("p (n b u) -> p n b u", n=UNITS, u=2)
            permuted = [n for units in permuted_units(r) for n in units]
            for pair in range(UNITS // 2):
                xt = psum.tile([P, 2, 2, P], F32, tag="xt")
                for a in range(2):
                    n = 2 * pair + a
                    for u in range(2):
                        if n in permuted:
                            column = perm_of[r][:, n, u, :]
                        else:
                            column = words_of(r, n, 1)[:, 0, u:PASS_WORDS:2]
                        nc.tensor.transpose(xt[:, a, u, :], column, ident[:])
                nc.scalar.copy(
                    out=grouped_words[:, 2 * pair : 2 * pair + 2, :, :],
                    in_=xt[:].rearrange("p a u b -> p a b u"),
                )
            hgrouped_of[r] = hgrouped

        def quantise_units(r, first, count):
            if first == 0:
                hcodes = hq_pool.tile([P, UNITS * P], U32, tag="hcodes", align_bytes=64)
                hscales = hq_pool.tile([P, UNITS * P], U8, tag="hscales", align_bytes=64)
                hq_of[r] = (hcodes, hscales)
            hcodes, hscales = hq_of[r]
            cols = slice(first * P, (first + count) * P)
            nc.vector.quantize_mx(
                out=hcodes[:, cols].bitcast(FP8X4),
                scales=hscales[:, cols],
                in_=hgrouped_of[r][:, first * K_PASS : (first + count) * K_PASS],
            )

        acc = {}

        def multiply_units(r, first, count):
            first_token, n_tokens, first_pass = rounds[r]
            n_cols = n_tokens * P
            hcodes, hscales = hq_of[r]
            if first_pass == 0 and first == 0:
                for j in range(C_TILES):
                    acc[j] = psum.tile([P, n_cols], F32, tag="acc", name="acc%d" % j)
            for j in range(C_TILES):
                for local_pass in range(first // n_tokens, (first + count) // n_tokens):
                    g = first_pass + local_pass
                    cols = slice(local_pass * n_cols, (local_pass + 1) * n_cols)
                    nc.tensor.matmul_mx(
                        out=acc[j][:],
                        lhsT=w_codes[:, g, j * P : (j + 1) * P].bitcast(FP8X4),
                        lhsT_scale=w_scales[:, g, j * P : (j + 1) * P],
                        rhs=hcodes[:, cols].bitcast(FP8X4),
                        rhs_scale=hscales[:, cols],
                        start=(g == 0),
                        stop=(g == PASSES - 1),
                    )

        def square_bank(j, square):
            nc.scalar.activation(
                out=square, in_=acc[j][:], func=ACT.Square, bias=tok_bias_third[:, j : j + 1], scale=1.0 / 3.0
            )

        def cube_bank(j, square, cube):
            nc.vector.scalar_tensor_tensor(
                out=cube, in0=acc[j][:], scalar=tok_bias[:, j : j + 1], in1=square, op0=ALU.add, op1=ALU.mult
            )

        def add_cubes(cubes, half, first):
            part = cubes[:, :, 2 * half * P : 2 * (half + 1) * P]
            if first:
                nc.vector.tensor_scalar(out=cube_sum[:], in0=part, scalar1=MIN_CUBE, scalar2=None, op0=ALU.max)
            else:
                nc.vector.scalar_tensor_tensor(
                    out=cube_sum[:], in0=part, scalar=MIN_CUBE, in1=cube_sum[:], op0=ALU.max, op1=ALU.add
                )

        transpose_bias()
        for piece in pieces_of_round(0):
            regroup_piece(piece)
        for piece in pieces_of_round(0):
            quantise_piece(piece)

        group = 0
        cubes = None
        closed_at = 0

        for r in range(n_rounds):
            transpose_round(r)
            if r + LOOKAHEAD < n_rounds:
                permute_round(r + LOOKAHEAD)
            if r >= 1:
                multiply_units(r - 1, 0, UNITS)
            if r < n_rounds - 1:
                quantise_units(r, 0, UNITS)
            else:
                quantise_units(r, 0, UNITS // 2)
                add_cubes(cubes, 1, first=False)
                quantise_units(r, UNITS // 2, UNITS // 2)
            if r >= 1 and rounds[r][2] == 0:
                cubes = cube_pool.tile([P, C_TILES, BANK], F32, tag="cubes")
                closed_at = r
                for j in range(C_TILES):
                    square = work.tile([P, BANK], F32, tag="square")
                    square_bank(j, square[:])
                    cube_bank(j, square[:], cubes[:, j, :])
                group += 1
                if group == 2:
                    add_cubes(cubes, 0, first=False)
            new_pieces = pieces_of_round(r + 1)
            for piece in new_pieces:
                regroup_piece(piece)
            if group == 1 and r - closed_at in (1, 2):
                half = r - closed_at - 1
                add_cubes(cubes, half, first=(half == 0))
            for piece in new_pieces:
                quantise_piece(piece)
            transposed.add(r)
            issue_loads()

        for half in range(2):
            multiply_units(n_rounds - 1, half * (UNITS // 2), UNITS // 2)
        both = const.tile([P, C_TILES, P], F32)
        nc.vector.tensor_tensor(out=both[:], in0=cube_sum[:, :, 0:P], in1=cube_sum[:, :, P : 2 * P], op=ALU.add)
        last_square = const.tile([P, C_TILES, P], F32)
        last = const.tile([P, C_TILES, P], F32)
        mean = const.tile([P, C_TILES, P], F32)
        log_mean = const.tile([P, C_TILES, P], F32)
        for j in range(C_TILES + 1):
            if j < C_TILES:
                square_bank(j, last_square[:, j, :])
                cube_bank(j, last_square[:, j, :], last[:, j, :])
            if j >= 1:
                nc.vector.scalar_tensor_tensor(
                    out=mean[:, j - 1, :],
                    in0=last[:, j - 1, :],
                    scalar=MIN_CUBE,
                    in1=both[:, j - 1, :],
                    op0=ALU.max,
                    op1=ALU.add,
                )
        nc.scalar.activation(out=log_mean[:, 0:2, :], in_=mean[:, 0:2, :], func=ACT.Ln)
        nc.scalar.activation(out=log_mean[:, 2, :], in_=mean[:, 2, :], func=ACT.Ln)
        nc.scalar.activation(out=log_mean[:, 3, :], in_=mean[:, 3, :], func=ACT.Ln)
        g_grouped = const.tile([P, P, PACK], BF16, align_bytes=64)
        nc.scalar.activation(
            out=g_grouped[:], in_=log_mean[:].rearrange("p j b -> p b j"), func=ACT.Exp, scale=1.0 / 3.0
        )
        g_codes = const.tile([P, P], U32, align_bytes=64)
        g_scales = const.tile([P, P], U8, align_bytes=64)
        nc.vector.quantize_mx(
            out=g_codes[:].bitcast(FP8X4), scales=g_scales[:], in_=g_grouped[:].rearrange("p b j -> p (b j)")
        )

        halves = [raw_pool.tile([P, CLASSES // 2], F32, tag="raw", name="d%d" % i) for i in range(2)]

        def d(n):
            half, bank = divmod(n, D_BANKS // 2)
            return halves[half][:, bank * BANK : (bank + 1) * BANK]

        squares = const.tile([P, D_BANKS], F32)
        for n in range(D_BANKS):
            cols = slice(n * BANK, (n + 1) * BANK)
            d_bank = psum.tile([P, BANK], F32, tag=("acc" if n < 4 else "xt"), name="d_bank")
            nc.tensor.matmul_mx(
                out=d_bank[:],
                lhsT=g_codes[:].bitcast(FP8X4),
                lhsT_scale=g_scales[:],
                rhs=hw_codes[:, n, :].bitcast(FP8X4),
                rhs_scale=hw_scales[:, n, :],
                start=True,
                stop=True,
            )
            nc.vector.tensor_tensor(out=d(n), in0=d_bank[:], in1=head_bias[:, cols], op=ALU.add)
            d2 = work.tile([P, BANK], F32, tag="square")
            nc.scalar.activation(out=d2[:], in_=d(n), func=ACT.Square, accum_out=squares[:, n : n + 1])
        norm2 = const.tile([P, 1], F32)
        nc.vector.tensor_reduce(out=norm2[:], in_=squares[:], axis=AX.X, op=ALU.add)
        safe2 = const.tile([P, 1], F32)
        nc.vector.tensor_scalar(out=safe2[:], in0=norm2[:], scalar1=EPS_NORM**2, scalar2=None, op0=ALU.max)
        inv_norm = const.tile([P, 1], F32)
        nc.gpsimd.tensor_tensor(out=inv_norm[:], in0=safe2[:], in1=minus_half[:], op=ALU.pow)
        for n in range(D_BANKS):
            cols = slice(n * BANK, (n + 1) * BANK)
            if n % 3 == 1:
                nc.scalar.activation(out=d(n), in_=d(n), func=ACT.Copy, scale=inv_norm[:])
            else:
                nc.vector.tensor_scalar(
                    out=d(n), in0=d(n), scalar1=inv_norm[:], scalar2=None, op0=ALU.mult
                )
        for n in (0, 2, 1, 3, 5, 4, 6, 7):
            cols = slice(n * BANK, (n + 1) * BANK)
            nc.sync.dma_start(out=out[:, cols], in_=d(n))
